import numpy as np
import ml_dtypes


def mxq(x, axis, fmt="e4m3"):
    dtype, down = {"e4m3": (ml_dtypes.float8_e4m3fn, 7), "e5m2": (ml_dtypes.float8_e5m2, 14)}[fmt]
    v = np.moveaxis(np.asarray(x, np.float32).astype(ml_dtypes.bfloat16).astype(np.float64), axis, -1)
    blocks = v.reshape(v.shape[:-1] + (-1, 32))
    amax = np.abs(blocks).max(-1, keepdims=True)
    byte = np.maximum(np.where(amax > 0, np.frexp(amax)[1] - 1 + 127, 0) - down, 1)
    scale = np.exp2(byte - 127.0)
    codes = (blocks / scale).astype(np.float32).astype(dtype).astype(np.float64)
    return np.moveaxis((codes * scale).reshape(v.shape), -1, axis)


WIDE = False


def mx_kscale(k):
    if not WIDE:
        return np.ones(k)
    levels = np.array([10, -10, 5, -5, 0])
    a = np.random.permutation(np.resize(levels, k // 512 * 4)).reshape(k // 512, 4)
    idx = np.arange(k)
    return np.exp2(a[idx // 512, idx % 128 // 32])


BF16 = ml_dtypes.bfloat16


def bf(x):
    return np.asarray(x, np.float32).astype(BF16)


def f64(x):
    return np.asarray(x).astype(np.float64)


E2M1 = np.array([0.0, 0.5, 1.0, 1.5, 2.0, 3.0, 4.0, 6.0, -0.0, -0.5, -1.0, -1.5, -2.0, -3.0, -4.0, -6.0])


def pack_weight(w, fmt):
    k, n = w.shape
    w = f64(bf(w)).reshape(k // 32, 32, n)
    amax = np.abs(w).max(1)
    if fmt == "e4m3":
        byte = np.frexp(amax)[1] - 1 + 127 - 7
    else:
        mant, ex = np.frexp(amax / 6.0)
        byte = np.where(mant > 0.5, ex, ex - 1) + 127
    byte = np.clip(np.where(amax > 0, byte, 1), 1, 254)
    scaled = (w * np.exp2(127.0 - byte)[:, None, :]).reshape(k, n).astype(np.float32)
    by_word = np.ascontiguousarray(scaled.reshape(k // 512, 128, 4, n).transpose(0, 1, 3, 2))
    if fmt == "e4m3":
        words = by_word.astype(ml_dtypes.float8_e4m3fn).view(np.uint8)
    else:
        c = by_word.astype(ml_dtypes.float4_e2m1fn).view(np.uint8) & 0xF
        words = c[..., 0::2] | (c[..., 1::2] << 4)
    return np.ascontiguousarray(words), np.ascontiguousarray(byte.astype(np.uint8).reshape(k // 512, 16, n))


def unpack_weight(words, scales, fmt):
    g, p, n, _ = words.shape
    if fmt == "e4m3":
        vals = np.ascontiguousarray(words).view(ml_dtypes.float8_e4m3fn).astype(np.float64)
    else:
        nib = np.empty((g, p, n, 4), np.uint8)
        nib[..., 0::2] = words & 0xF
        nib[..., 1::2] = words >> 4
        vals = E2M1[nib]
    vals = vals * np.repeat(np.exp2(scales.astype(np.float64) - 127.0), 8, axis=1)[..., None]
    return vals.transpose(0, 1, 3, 2).reshape(g * 512, n)

def pack4(w):
    words, scales = pack_weight(w, "e2m1")
    return words.reshape(words.shape[0], 128, -1), scales


def unpack4(words, scales):
    return unpack_weight(words.reshape(words.shape[0], 128, -1, 2), scales, "e2m1")


B, S, H, E, D, TRAIN_LEN = 1, 256, 512, 768, 128, 512


def silu(v):
    return v / (1.0 + np.exp(-v))


def apply_rotary(x, sin, cos):
    x1, x2 = x[..., 0::2], x[..., 1::2]
    return np.concatenate([x1 * cos - x2 * sin, x1 * sin + x2 * cos], axis=-1)


def setup_inputs():
    s = mx_kscale(H)
    pos = np.arange(S)[:, None]
    inv = np.exp(-np.arange(0, D, 2) / D * np.log(10000.0))
    ang = pos * inv[None, :]
    hidden_states = bf(np.random.standard_normal((B, S, H)) * s)
    words, scales = pack4(np.random.standard_normal((H, 2 * E + D)) / np.sqrt(H) / s[:, None])
    return {"hidden_states": hidden_states,
            "sin": bf(np.sin(ang)[None]),
            "cos": bf(np.cos(ang)[None]),
            "W_i_words": words,
            "W_i_scales": scales,
            "q_scale": bf(1.0 + 0.1 * np.random.standard_normal(D)),
            "k_scale": bf(1.0 + 0.1 * np.random.standard_normal(D))}


def reference(hidden_states, sin, cos, W_i_words, W_i_scales, q_scale, k_scale):
    x = silu(mxq(f64(hidden_states), 2, "e4m3") @ unpack4(W_i_words, W_i_scales))
    u, v, qk = np.split(x, [E, 2 * E], axis=-1)
    sn, cs = f64(sin), f64(cos)
    q = apply_rotary(qk * f64(q_scale), sn, cs)
    k = apply_rotary(qk * f64(k_scale), sn, cs)
    return u, v, q, k

@@ -1,0 +1,176 @@
+from contextlib import ExitStack
+
+import concourse.mybir as mybir
+from concourse.masks import make_identity
+
+F32 = mybir.dt.float32
+BF16 = mybir.dt.bfloat16
+I32 = mybir.dt.int32
+U32 = mybir.dt.uint32
+U8 = mybir.dt.uint8
+FP8X4 = mybir.dt.float8_e4m3fn_x4
+FP4X4 = mybir.dt.float4_e2m1fn_x4
+SILU = mybir.ActivationFunctionType.Silu
+MULT = mybir.AluOpType.mult
+ADD = mybir.AluOpType.add
+SUBTRACT = mybir.AluOpType.subtract
+
+P = 128
+S = 256
+H = 512
+E = 768
+D = 128
+HALF = D // 2
+N_ALL = 2 * E + D
+TT = S // P
+BANK = 512
+PIECES = ((0, 512), (512, 256))
+
+FLOPS = 2 * S * H * N_ALL
+
+
+def tile_gatedattentionunit_pa_s_kernel(
+    tc, hidden_states, sin, cos, W_i_words, W_i_scales, q_scale, k_scale, out_0, out_1, out_2, out_3
+):
+    nc = tc.nc
+    with ExitStack() as ctx:
+        ctx.enter_context(tc.manual_schedule())
+        keep = ctx.enter_context(tc.tile_pool(name="keep", bufs=1))
+        stages = ctx.enter_context(tc.tile_pool(name="stages", bufs=4))
+        psum_once = ctx.enter_context(tc.psum_pool(name="psum_once", bufs=1))
+        psum_acc = ctx.enter_context(tc.psum_pool(name="psum_acc", bufs=4))
+
+        x_sb = keep.tile([P, TT, H], BF16)
+        nc.sync.dma_start(out=x_sb[:], in_=hidden_states[0].rearrange("(p t) k -> p t k", t=TT))
+
+        w_scales = keep.tile([P, N_ALL], U8, align_bytes=64)
+        nc.vector.memset(w_scales[:].bitcast(I32), 0)
+        for quad in range(4):
+            nc.sync.dma_start(
+                out=w_scales[32 * quad : 32 * quad + 4, :].bitcast(I32),
+                in_=W_i_scales[0, 4 * quad : 4 * quad + 4, :].bitcast(I32),
+            )
+        w_words = keep.tile([P, 2 * N_ALL], U8, align_bytes=64)
+        nc.sync.dma_start(out=w_words[:].bitcast(I32), in_=W_i_words[0].bitcast(I32))
+
+        gain_rows = keep.tile([P, 2 * D], BF16)
+        nc.vector.memset(gain_rows[:], 0.0)
+        ones = keep.tile([P, P], BF16)
+        nc.vector.memset(ones[:], 1.0)
+        nc.scalar.dma_start(out=gain_rows[0:1, 0:D], in_=q_scale.rearrange("(o c) -> o c", o=1))
+        nc.scalar.dma_start(out=gain_rows[0:1, D : 2 * D], in_=k_scale.rearrange("(o c) -> o c", o=1))
+        warm = keep.tile([P, 1], F32)
+        nc.scalar.activation(out=warm[:], in_=ones[:, 0:1], func=SILU)
+
+        ident = keep.tile([P, P], F32)
+        make_identity(nc, ident[:])
+        cos_sb = keep.tile([P, TT, HALF], BF16)
+        sin_sb = keep.tile([P, TT, HALF], BF16)
+        nc.gpsimd.dma_start(out=cos_sb[:], in_=cos[0].rearrange("(p t) c -> p t c", t=TT))
+        nc.gpsimd.dma_start(out=sin_sb[:], in_=sin[0].rearrange("(p t) c -> p t c", t=TT))
+
+        x_t = [psum_once.tile([P, 2, P], F32, name="x_t%d" % t) for t in range(TT)]
+        for t in range(TT):
+            x_words = x_sb[:, t, :].bitcast(F32)
+            for u in range(2):
+                nc.tensor.transpose(x_t[t][:, u, :], x_words[:, u : H // 2 : 2], ident[:])
+        gains = psum_once.tile([P, 2, 2, HALF], F32)
+        nc.tensor.matmul(
+            out=gains[:],
+            lhsT=ones[:],
+            rhs=gain_rows[:].rearrange("p (s c e) -> p s e c", s=2, e=2),
+            start=True,
+            stop=True,
+        )
+        grouped = [keep.tile([P, 4 * P], BF16, name="grouped%d" % t, align_bytes=64) for t in range(TT)]
+        copy_out = (nc.vector.tensor_copy, nc.scalar.copy)
+        for t in range(TT):
+            copy_out[t](
+                out=grouped[t][:].bitcast(F32).rearrange("p (r u) -> p r u", u=2),
+                in_=x_t[t][:].rearrange("p u r -> p r u"),
+            )
+        x_codes = keep.tile([P, TT, P], U32, align_bytes=64)
+        x_scales = keep.tile([P, TT, P], U8, align_bytes=64)
+        for t in range(TT):
+            nc.vector.quantize_mx(out=x_codes[:, t, :].bitcast(FP8X4), scales=x_scales[:, t, :], in_=grouped[t][:])
+
+        def project(t, first, width):
+            acc = psum_acc.tile([P, BANK], F32, tag="acc")
+            nc.tensor.matmul_mx(
+                out=acc[:, :width],
+                lhsT=x_codes[:, t, :].bitcast(FP8X4),
+                lhsT_scale=x_scales[:, t, :],
+                rhs=w_words[:, 2 * first : 2 * (first + width)].bitcast(FP4X4),
+                rhs_scale=w_scales[:, first : first + width],
+                start=True,
+                stop=True,
+            )
+            return acc
+
+        def gated(t, first, out):
+            stage = stages.tile([P, E], F32, tag="stage")
+            for c0, width in PIECES:
+                acc = project(t, first + c0, width)
+                nc.scalar.activation(out=stage[:, c0 : c0 + width], in_=acc[:, :width], func=SILU)
+            nc.sync.dma_start(out=out[0].rearrange("(p t) c -> p t c", t=TT)[:, t, :], in_=stage[:])
+
+        gated(0, 0, out_0)
+
+        qk_acc = psum_once.tile([P, TT, D], F32)
+        for t in range(TT):
+            nc.tensor.matmul_mx(
+                out=qk_acc[:, t, :],
+                lhsT=x_codes[:, t, :].bitcast(FP8X4),
+                lhsT_scale=x_scales[:, t, :],
+                rhs=w_words[:, 2 * 2 * E : 2 * N_ALL].bitcast(FP4X4),
+                rhs_scale=w_scales[:, 2 * E : N_ALL],
+                start=True,
+                stop=True,
+            )
+        qk = keep.tile([P, TT, 2, HALF], F32)
+        nc.scalar.activation(out=qk[:], in_=qk_acc[:].rearrange("p t (c e) -> p t e c", e=2), func=SILU)
+
+        gain_all = gains[:].rearrange("p s e c -> p (s e) c").unsqueeze(1).to_broadcast([P, TT, 4, HALF])
+        gain_cos = keep.tile([P, TT, 2, 2, HALF], F32)
+        gain_sin = keep.tile([P, TT, 2, 2, HALF], F32)
+        for table, angle in ((gain_cos, cos_sb), (gain_sin, sin_sb)):
+            nc.vector.tensor_tensor(
+                out=table[:].rearrange("p t s e c -> p t (s e) c"),
+                in0=gain_all,
+                in1=angle[:].unsqueeze(2).to_broadcast([P, TT, 4, HALF]),
+                op=MULT,
+            )
+
+        gated(0, E, out_1)
+
+        qk_both = qk[:].rearrange("p t e c -> p t (e c)").unsqueeze(2).to_broadcast([P, TT, 2, D])
+        y_cos = keep.tile([P, TT, 2, 2, HALF], F32)
+        y_sin = keep.tile([P, TT, 2, 2, HALF], F32)
+        for product, table in ((y_cos, gain_cos), (y_sin, gain_sin)):
+            nc.vector.tensor_tensor(
+                out=product[:].rearrange("p t s e c -> p t s (e c)"),
+                in0=qk_both,
+                in1=table[:].rearrange("p t s e c -> p t s (e c)"),
+                op=MULT,
+            )
+        rotated = keep.tile([P, 2, TT, 2, HALF], F32)
+        nc.vector.tensor_tensor(
+            out=rotated[:, :, :, 0, :].rearrange("p s t c -> p t s c"),
+            in0=y_cos[:, :, :, 0, :],
+            in1=y_sin[:, :, :, 1, :],
+            op=SUBTRACT,
+        )
+        nc.vector.tensor_tensor(
+            out=rotated[:, :, :, 1, :].rearrange("p s t c -> p t s c"),
+            in0=y_sin[:, :, :, 0, :],
+            in1=y_cos[:, :, :, 1, :],
+            op=ADD,
+        )
+
+        gated(1, 0, out_0)
+        for s, out in enumerate((out_2, out_3)):
+            nc.sync.dma_start(
+                out=out[0].rearrange("(p t) c -> p (t c)", t=TT),
+                in_=rotated[:, s].rearrange("p t h c -> p (t h c)"),
+            )
+        gated(1, E, out_1)

@@ -24,7 +24,8 @@ HALF = D // 2
 N_ALL = 2 * E + D
 TT = S // P
 BANK = 512
-PIECES = ((0, 512), (512, 256))
+NARROW_FIRST = ((0, 256), (256, 512))
+NARROW_LAST = ((0, 512), (512, 256))
 
 FLOPS = 2 * S * H * N_ALL
 
@@ -36,7 +37,7 @@ def tile_gatedattentionunit_pa_s_kernel(
     with ExitStack() as ctx:
         ctx.enter_context(tc.manual_schedule())
         keep = ctx.enter_context(tc.tile_pool(name="keep", bufs=1))
-        stages = ctx.enter_context(tc.tile_pool(name="stages", bufs=4))
+        stages = ctx.enter_context(tc.tile_pool(name="stages", bufs=8))
         psum_once = ctx.enter_context(tc.psum_pool(name="psum_once", bufs=1))
         psum_acc = ctx.enter_context(tc.psum_pool(name="psum_acc", bufs=4))
 
@@ -62,12 +63,13 @@ def tile_gatedattentionunit_pa_s_kernel(
         warm = keep.tile([P, 1], F32)
         nc.scalar.activation(out=warm[:], in_=ones[:, 0:1], func=SILU)
 
-        ident = keep.tile([P, P], F32)
-        make_identity(nc, ident[:])
         cos_sb = keep.tile([P, TT, HALF], BF16)
         sin_sb = keep.tile([P, TT, HALF], BF16)
         nc.gpsimd.dma_start(out=cos_sb[:], in_=cos[0].rearrange("(p t) c -> p t c", t=TT))
         nc.gpsimd.dma_start(out=sin_sb[:], in_=sin[0].rearrange("(p t) c -> p t c", t=TT))
+        ident = keep.tile([P, P], F32)
+        nc.vector.memset(ident[:], 0.0)
+        make_identity(nc, ident[:], nomemset=True)
 
         x_t = [psum_once.tile([P, 2, P], F32, name="x_t%d" % t) for t in range(TT)]
         for t in range(TT):
@@ -107,14 +109,15 @@ def tile_gatedattentionunit_pa_s_kernel(
             )
             return acc
 
-        def gated(t, first, out):
-            stage = stages.tile([P, E], F32, tag="stage")
-            for c0, width in PIECES:
+        def gated(t, first, pieces, out):
+            rows = out[0].rearrange("(p t) c -> p t c", t=TT)[:, t, :]
+            for c0, width in pieces:
                 acc = project(t, first + c0, width)
-                nc.scalar.activation(out=stage[:, c0 : c0 + width], in_=acc[:, :width], func=SILU)
-            nc.sync.dma_start(out=out[0].rearrange("(p t) c -> p t c", t=TT)[:, t, :], in_=stage[:])
+                stage = stages.tile([P, BANK], F32, tag="stage")
+                nc.scalar.activation(out=stage[:, :width], in_=acc[:, :width], func=SILU)
+                nc.sync.dma_start(out=rows[:, c0 : c0 + width], in_=stage[:, :width])
 
-        gated(0, 0, out_0)
+        gated(0, 0, NARROW_FIRST, out_0)
 
         qk_acc = psum_once.tile([P, TT, D], F32)
         for t in range(TT):
@@ -141,7 +144,7 @@ def tile_gatedattentionunit_pa_s_kernel(
                 op=MULT,
             )
 
-        gated(0, E, out_1)
+        gated(0, E, NARROW_LAST, out_1)
 
         qk_both = qk[:].rearrange("p t e c -> p t (e c)").unsqueeze(2).to_broadcast([P, TT, 2, D])
         y_cos = keep.tile([P, TT, 2, 2, HALF], F32)
@@ -167,10 +170,10 @@ def tile_gatedattentionunit_pa_s_kernel(
             op=ADD,
         )
 
-        gated(1, 0, out_0)
+        gated(1, 0, NARROW_FIRST, out_0)
         for s, out in enumerate((out_2, out_3)):
             nc.sync.dma_start(
                 out=out[0].rearrange("(p t) c -> p (t c)", t=TT),
                 in_=rotated[:, s].rearrange("p t h c -> p (t h c)"),
             )
-        gated(1, E, out_1)
+        gated(1, E, NARROW_LAST, out_1)

@@ -24,8 +24,7 @@ HALF = D // 2
 N_ALL = 2 * E + D
 TT = S // P
 BANK = 512
-NARROW_FIRST = ((0, 256), (256, 512))
-NARROW_LAST = ((0, 512), (512, 256))
+NARROW = E - BANK
 
 FLOPS = 2 * S * H * N_ALL
 
@@ -41,9 +40,12 @@ def tile_gatedattentionunit_pa_s_kernel(
         psum_once = ctx.enter_context(tc.psum_pool(name="psum_once", bufs=1))
         psum_acc = ctx.enter_context(tc.psum_pool(name="psum_acc", bufs=4))
 
-        x_sb = keep.tile([P, TT, H], BF16)
-        nc.sync.dma_start(out=x_sb[:], in_=hidden_states[0].rearrange("(p t) k -> p t k", t=TT))
-
+        x_rows = hidden_states[0].rearrange("(p t) k -> p t k", t=TT)
+        x_sb = [keep.tile([P, H], BF16, name="x_sb%d" % t) for t in range(TT)]
+        for t in range(TT):
+            nc.sync.dma_start(out=x_sb[t][:], in_=x_rows[:, t, :])
+        w_words = keep.tile([P, 2 * N_ALL], U8, align_bytes=64)
+        nc.sync.dma_start(out=w_words[:, 2 * E :].bitcast(I32), in_=W_i_words[0, :, 2 * E :].bitcast(I32))
         w_scales = keep.tile([P, N_ALL], U8, align_bytes=64)
         nc.vector.memset(w_scales[:].bitcast(I32), 0)
         for quad in range(4):
@@ -51,43 +53,32 @@ def tile_gatedattentionunit_pa_s_kernel(
                 out=w_scales[32 * quad : 32 * quad + 4, :].bitcast(I32),
                 in_=W_i_scales[0, 4 * quad : 4 * quad + 4, :].bitcast(I32),
             )
-        w_words = keep.tile([P, 2 * N_ALL], U8, align_bytes=64)
-        nc.sync.dma_start(out=w_words[:].bitcast(I32), in_=W_i_words[0].bitcast(I32))
-
+        nc.sync.dma_start(out=w_words[:, : 2 * E].bitcast(I32), in_=W_i_words[0, :, : 2 * E].bitcast(I32))
         gain_rows = keep.tile([P, 2 * D], BF16)
         nc.vector.memset(gain_rows[:], 0.0)
         ones = keep.tile([P, P], BF16)
         nc.vector.memset(ones[:], 1.0)
-        nc.scalar.dma_start(out=gain_rows[0:1, 0:D], in_=q_scale.rearrange("(o c) -> o c", o=1))
-        nc.scalar.dma_start(out=gain_rows[0:1, D : 2 * D], in_=k_scale.rearrange("(o c) -> o c", o=1))
+        nc.sync.dma_start(out=gain_rows[0:1, 0:D], in_=q_scale.rearrange("(o c) -> o c", o=1))
+        nc.sync.dma_start(out=gain_rows[0:1, D : 2 * D], in_=k_scale.rearrange("(o c) -> o c", o=1))
+
         warm = keep.tile([P, 1], F32)
         nc.scalar.activation(out=warm[:], in_=ones[:, 0:1], func=SILU)
 
+        ident = keep.tile([P, P], F32)
+        make_identity(nc, ident[:])
         cos_sb = keep.tile([P, TT, HALF], BF16)
         sin_sb = keep.tile([P, TT, HALF], BF16)
         nc.gpsimd.dma_start(out=cos_sb[:], in_=cos[0].rearrange("(p t) c -> p t c", t=TT))
         nc.gpsimd.dma_start(out=sin_sb[:], in_=sin[0].rearrange("(p t) c -> p t c", t=TT))
-        ident = keep.tile([P, P], F32)
-        nc.vector.memset(ident[:], 0.0)
-        make_identity(nc, ident[:], nomemset=True)
 
         x_t = [psum_once.tile([P, 2, P], F32, name="x_t%d" % t) for t in range(TT)]
         for t in range(TT):
-            x_words = x_sb[:, t, :].bitcast(F32)
+            x_words = x_sb[t][:].bitcast(F32)
             for u in range(2):
                 nc.tensor.transpose(x_t[t][:, u, :], x_words[:, u : H // 2 : 2], ident[:])
-        gains = psum_once.tile([P, 2, 2, HALF], F32)
-        nc.tensor.matmul(
-            out=gains[:],
-            lhsT=ones[:],
-            rhs=gain_rows[:].rearrange("p (s c e) -> p s e c", s=2, e=2),
-            start=True,
-            stop=True,
-        )
         grouped = [keep.tile([P, 4 * P], BF16, name="grouped%d" % t, align_bytes=64) for t in range(TT)]
-        copy_out = (nc.vector.tensor_copy, nc.scalar.copy)
         for t in range(TT):
-            copy_out[t](
+            nc.scalar.copy(
                 out=grouped[t][:].bitcast(F32).rearrange("p (r u) -> p r u", u=2),
                 in_=x_t[t][:].rearrange("p u r -> p r u"),
             )
@@ -96,10 +87,9 @@ def tile_gatedattentionunit_pa_s_kernel(
         for t in range(TT):
             nc.vector.quantize_mx(out=x_codes[:, t, :].bitcast(FP8X4), scales=x_scales[:, t, :], in_=grouped[t][:])
 
-        def project(t, first, width):
-            acc = psum_acc.tile([P, BANK], F32, tag="acc")
+        def project(acc, t, first, width):
             nc.tensor.matmul_mx(
-                out=acc[:, :width],
+                out=acc,
                 lhsT=x_codes[:, t, :].bitcast(FP8X4),
                 lhsT_scale=x_scales[:, t, :],
                 rhs=w_words[:, 2 * first : 2 * (first + width)].bitcast(FP4X4),
@@ -107,53 +97,50 @@ def tile_gatedattentionunit_pa_s_kernel(
                 start=True,
                 stop=True,
             )
-            return acc
 
-        def gated(t, first, pieces, out):
-            rows = out[0].rearrange("(p t) c -> p t c", t=TT)[:, t, :]
-            for c0, width in pieces:
-                acc = project(t, first + c0, width)
-                stage = stages.tile([P, BANK], F32, tag="stage")
-                nc.scalar.activation(out=stage[:, :width], in_=acc[:, :width], func=SILU)
-                nc.sync.dma_start(out=rows[:, c0 : c0 + width], in_=stage[:, :width])
+        def gated(t, half, c0, width):
+            acc = psum_acc.tile([P, BANK], F32, tag="acc")
+            project(acc[:, :width], t, half * E + c0, width)
+            stage = stages.tile([P, BANK], F32, tag="stage")
+            nc.scalar.activation(out=stage[:, :width], in_=acc[:, :width], func=SILU)
+            rows = (out_0, out_1)[half][0].rearrange("(p t) c -> p t c", t=TT)
+            nc.sync.dma_start(out=rows[:, t, c0 : c0 + width], in_=stage[:, :width])
 
-        gated(0, 0, NARROW_FIRST, out_0)
+        gated(0, 1, 0, NARROW)
 
         qk_acc = psum_once.tile([P, TT, D], F32)
         for t in range(TT):
-            nc.tensor.matmul_mx(
-                out=qk_acc[:, t, :],
-                lhsT=x_codes[:, t, :].bitcast(FP8X4),
-                lhsT_scale=x_scales[:, t, :],
-                rhs=w_words[:, 2 * 2 * E : 2 * N_ALL].bitcast(FP4X4),
-                rhs_scale=w_scales[:, 2 * E : N_ALL],
-                start=True,
-                stop=True,
-            )
+            project(qk_acc[:, t, :], t, 2 * E, D)
         qk = keep.tile([P, TT, 2, HALF], F32)
         nc.scalar.activation(out=qk[:], in_=qk_acc[:].rearrange("p t (c e) -> p t e c", e=2), func=SILU)
 
-        gain_all = gains[:].rearrange("p s e c -> p (s e) c").unsqueeze(1).to_broadcast([P, TT, 4, HALF])
-        gain_cos = keep.tile([P, TT, 2, 2, HALF], F32)
-        gain_sin = keep.tile([P, TT, 2, 2, HALF], F32)
-        for table, angle in ((gain_cos, cos_sb), (gain_sin, sin_sb)):
-            nc.vector.tensor_tensor(
-                out=table[:].rearrange("p t s e c -> p t (s e) c"),
-                in0=gain_all,
-                in1=angle[:].unsqueeze(2).to_broadcast([P, TT, 4, HALF]),
-                op=MULT,
-            )
+        gated(0, 1, NARROW, BANK)
+        gated(0, 0, 0, BANK)
 
-        gated(0, E, NARROW_LAST, out_1)
+        gains = psum_once.tile([P, 2, 2, HALF], F32)
+        nc.tensor.matmul(
+            out=gains[:],
+            lhsT=ones[:],
+            rhs=gain_rows[:].rearrange("p (s c e) -> p s e c", s=2, e=2),
+            start=True,
+            stop=True,
+        )
 
-        qk_both = qk[:].rearrange("p t e c -> p t (e c)").unsqueeze(2).to_broadcast([P, TT, 2, D])
         y_cos = keep.tile([P, TT, 2, 2, HALF], F32)
         y_sin = keep.tile([P, TT, 2, 2, HALF], F32)
-        for product, table in ((y_cos, gain_cos), (y_sin, gain_sin)):
+        gains_all = gains[:].rearrange("p s e c -> p s (e c)").unsqueeze(1).to_broadcast([P, TT, 2, D])
+        turned = []
+        for name, angle in (("qk_cos", cos_sb), ("qk_sin", sin_sb)):
+            product = keep.tile([P, TT, 2, HALF], F32, name=name)
             nc.vector.tensor_tensor(
-                out=product[:].rearrange("p t s e c -> p t s (e c)"),
-                in0=qk_both,
-                in1=table[:].rearrange("p t s e c -> p t s (e c)"),
+                out=product[:], in0=qk[:], in1=angle[:].unsqueeze(2).to_broadcast([P, TT, 2, HALF]), op=MULT
+            )
+            turned.append(product)
+        for y, product in zip((y_cos, y_sin), turned):
+            nc.vector.tensor_tensor(
+                out=y[:].rearrange("p t s e c -> p t s (e c)"),
+                in0=product[:].rearrange("p t e c -> p t (e c)").unsqueeze(2).to_broadcast([P, TT, 2, D]),
+                in1=gains_all,
                 op=MULT,
             )
         rotated = keep.tile([P, 2, TT, 2, HALF], F32)
@@ -170,10 +157,13 @@ def tile_gatedattentionunit_pa_s_kernel(
             op=ADD,
         )
 
-        gated(1, 0, NARROW_FIRST, out_0)
+        gated(0, 0, BANK, NARROW)
+        gated(1, 1, 0, NARROW)
+        gated(1, 1, NARROW, BANK)
+        gated(1, 0, 0, BANK)
         for s, out in enumerate((out_2, out_3)):
             nc.sync.dma_start(
                 out=out[0].rearrange("(p t) c -> p (t c)", t=TT),
                 in_=rotated[:, s].rearrange("p t h c -> p (t h c)"),
             )
-        gated(1, E, NARROW_LAST, out_1)
+        gated(1, 0, BANK, NARROW)

@@ -40,6 +40,15 @@ def tile_gatedattentionunit_pa_s_kernel(
         psum_once = ctx.enter_context(tc.psum_pool(name="psum_once", bufs=1))
         psum_acc = ctx.enter_context(tc.psum_pool(name="psum_acc", bufs=4))
 
+        warm_in = keep.tile([P, 1], F32)
+        nc.vector.memset(warm_in[:], 0.0)
+        warm = keep.tile([P, 1], F32)
+        nc.scalar.activation(out=warm[:], in_=warm_in[:], func=SILU)
+
+        ident = keep.tile([P, P], F32)
+        nc.vector.memset(ident[:], 0.0)
+        make_identity(nc, ident[:], nomemset=True)
+
         x_rows = hidden_states[0].rearrange("(p t) k -> p t k", t=TT)
         x_sb = [keep.tile([P, H], BF16, name="x_sb%d" % t) for t in range(TT)]
         for t in range(TT):
@@ -61,11 +70,6 @@ def tile_gatedattentionunit_pa_s_kernel(
         nc.sync.dma_start(out=gain_rows[0:1, 0:D], in_=q_scale.rearrange("(o c) -> o c", o=1))
         nc.sync.dma_start(out=gain_rows[0:1, D : 2 * D], in_=k_scale.rearrange("(o c) -> o c", o=1))
 
-        warm = keep.tile([P, 1], F32)
-        nc.scalar.activation(out=warm[:], in_=ones[:, 0:1], func=SILU)
-
-        ident = keep.tile([P, P], F32)
-        make_identity(nc, ident[:])
         cos_sb = keep.tile([P, TT, HALF], BF16)
         sin_sb = keep.tile([P, TT, HALF], BF16)
         nc.gpsimd.dma_start(out=cos_sb[:], in_=cos[0].rearrange("(p t) c -> p t c", t=TT))

@@ -25,6 +25,7 @@ N_ALL = 2 * E + D
 TT = S // P
 BANK = 512
 NARROW = E - BANK
+IDLE_PRODUCTS = 3
 
 FLOPS = 2 * S * H * N_ALL
 
@@ -44,6 +45,12 @@ def tile_gatedattentionunit_pa_s_kernel(
         nc.vector.memset(warm_in[:], 0.0)
         warm = keep.tile([P, 1], F32)
         nc.scalar.activation(out=warm[:], in_=warm_in[:], func=SILU)
+
+        zeros = keep.tile([P, P], F32)
+        nc.vector.memset(zeros[:], 0.0)
+        idle_acc = psum_acc.tile([P, BANK], F32, tag="acc")
+        for i in range(IDLE_PRODUCTS):
+            nc.tensor.matmul(out=idle_acc[:, :P], lhsT=zeros[:], rhs=zeros[:], start=True, stop=True)
 
         ident = keep.tile([P, P], F32)
         nc.vector.memset(ident[:], 0.0)

@@ -74,13 +74,12 @@ def tile_gatedattentionunit_pa_s_kernel(
         nc.vector.memset(gain_rows[:], 0.0)
         ones = keep.tile([P, P], BF16)
         nc.vector.memset(ones[:], 1.0)
-        nc.sync.dma_start(out=gain_rows[0:1, 0:D], in_=q_scale.rearrange("(o c) -> o c", o=1))
-        nc.sync.dma_start(out=gain_rows[0:1, D : 2 * D], in_=k_scale.rearrange("(o c) -> o c", o=1))
-
         cos_sb = keep.tile([P, TT, HALF], BF16)
         sin_sb = keep.tile([P, TT, HALF], BF16)
-        nc.gpsimd.dma_start(out=cos_sb[:], in_=cos[0].rearrange("(p t) c -> p t c", t=TT))
-        nc.gpsimd.dma_start(out=sin_sb[:], in_=sin[0].rearrange("(p t) c -> p t c", t=TT))
+        nc.sync.dma_start(out=cos_sb[:], in_=cos[0].rearrange("(p t) c -> p t c", t=TT))
+        nc.sync.dma_start(out=sin_sb[:], in_=sin[0].rearrange("(p t) c -> p t c", t=TT))
+        nc.sync.dma_start(out=gain_rows[0:1, 0:D], in_=q_scale.rearrange("(o c) -> o c", o=1))
+        nc.sync.dma_start(out=gain_rows[0:1, D : 2 * D], in_=k_scale.rearrange("(o c) -> o c", o=1))
 
         x_t = [psum_once.tile([P, 2, P], F32, name="x_t%d" % t) for t in range(TT)]
         for t in range(TT):

@@ -41,10 +41,9 @@ def tile_gatedattentionunit_pa_s_kernel(
         psum_once = ctx.enter_context(tc.psum_pool(name="psum_once", bufs=1))
         psum_acc = ctx.enter_context(tc.psum_pool(name="psum_acc", bufs=4))
 
-        warm_in = keep.tile([P, 1], F32)
-        nc.vector.memset(warm_in[:], 0.0)
-        warm = keep.tile([P, 1], F32)
-        nc.scalar.activation(out=warm[:], in_=warm_in[:], func=SILU)
+        ident = keep.tile([P, P], F32)
+        nc.vector.memset(ident[:], 0.0)
+        make_identity(nc, ident[:], nomemset=True)
 
         zeros = keep.tile([P, P], F32)
         nc.vector.memset(zeros[:], 0.0)
@@ -52,9 +51,10 @@ def tile_gatedattentionunit_pa_s_kernel(
         for i in range(IDLE_PRODUCTS):
             nc.tensor.matmul(out=idle_acc[:, :P], lhsT=zeros[:], rhs=zeros[:], start=True, stop=True)
 
-        ident = keep.tile([P, P], F32)
-        nc.vector.memset(ident[:], 0.0)
-        make_identity(nc, ident[:], nomemset=True)
+        warm_in = keep.tile([P, 1], F32)
+        nc.vector.memset(warm_in[:], 0.0)
+        warm = keep.tile([P, 1], F32)
+        nc.scalar.activation(out=warm[:], in_=warm_in[:], func=SILU)
 
         x_rows = hidden_states[0].rearrange("(p t) k -> p t k", t=TT)
         x_sb = [keep.tile([P, H], BF16, name="x_sb%d" % t) for t in range(TT)]
@@ -71,9 +71,9 @@ def tile_gatedattentionunit_pa_s_kernel(
             )
         nc.sync.dma_start(out=w_words[:, : 2 * E].bitcast(I32), in_=W_i_words[0, :, : 2 * E].bitcast(I32))
         gain_rows = keep.tile([P, 2 * D], BF16)
-        nc.vector.memset(gain_rows[:], 0.0)
+        nc.gpsimd.memset(gain_rows[:], 0.0)
         ones = keep.tile([P, P], BF16)
-        nc.vector.memset(ones[:], 1.0)
+        nc.gpsimd.memset(ones[:], 1.0)
         cos_sb = keep.tile([P, TT, HALF], BF16)
         sin_sb = keep.tile([P, TT, HALF], BF16)
         nc.sync.dma_start(out=cos_sb[:], in_=cos[0].rearrange("(p t) c -> p t c", t=TT))

@@ -41,15 +41,18 @@ def tile_gatedattentionunit_pa_s_kernel(
         psum_once = ctx.enter_context(tc.psum_pool(name="psum_once", bufs=1))
         psum_acc = ctx.enter_context(tc.psum_pool(name="psum_acc", bufs=4))
 
-        ident = keep.tile([P, P], F32)
-        nc.vector.memset(ident[:], 0.0)
-        make_identity(nc, ident[:], nomemset=True)
-
         zeros = keep.tile([P, P], F32)
         nc.vector.memset(zeros[:], 0.0)
         idle_acc = psum_acc.tile([P, BANK], F32, tag="acc")
         for i in range(IDLE_PRODUCTS):
             nc.tensor.matmul(out=idle_acc[:, :P], lhsT=zeros[:], rhs=zeros[:], start=True, stop=True)
+
+        w_scales = keep.tile([P, N_ALL], U8, align_bytes=64)
+        nc.vector.memset(w_scales[:].bitcast(I32), 0)
+
+        ident = keep.tile([P, P], F32)
+        nc.vector.memset(ident[:], 0.0)
+        make_identity(nc, ident[:], nomemset=True)
 
         warm_in = keep.tile([P, 1], F32)
         nc.vector.memset(warm_in[:], 0.0)
@@ -61,15 +64,20 @@ def tile_gatedattentionunit_pa_s_kernel(
         for t in range(TT):
             nc.sync.dma_start(out=x_sb[t][:], in_=x_rows[:, t, :])
         w_words = keep.tile([P, 2 * N_ALL], U8, align_bytes=64)
-        nc.sync.dma_start(out=w_words[:, 2 * E :].bitcast(I32), in_=W_i_words[0, :, 2 * E :].bitcast(I32))
-        w_scales = keep.tile([P, N_ALL], U8, align_bytes=64)
-        nc.vector.memset(w_scales[:].bitcast(I32), 0)
+
+        def load_codes(first, last):
+            nc.sync.dma_start(
+                out=w_words[:, 2 * first : 2 * last].bitcast(I32), in_=W_i_words[0, :, 2 * first : 2 * last].bitcast(I32)
+            )
+
+        load_codes(E, E + NARROW)
         for quad in range(4):
             nc.sync.dma_start(
                 out=w_scales[32 * quad : 32 * quad + 4, :].bitcast(I32),
                 in_=W_i_scales[0, 4 * quad : 4 * quad + 4, :].bitcast(I32),
             )
-        nc.sync.dma_start(out=w_words[:, : 2 * E].bitcast(I32), in_=W_i_words[0, :, : 2 * E].bitcast(I32))
+        load_codes(E + NARROW, N_ALL)
+        load_codes(0, E)
         gain_rows = keep.tile([P, 2 * D], BF16)
         nc.gpsimd.memset(gain_rows[:], 0.0)
         ones = keep.tile([P, P], BF16)

@@ -25,6 +25,7 @@ N_ALL = 2 * E + D
 TT = S // P
 BANK = 512
 NARROW = E - BANK
+DMA_ALIGN = 256
 IDLE_PRODUCTS = 3
 
 FLOPS = 2 * S * H * N_ALL
@@ -47,7 +48,7 @@ def tile_gatedattentionunit_pa_s_kernel(
         for i in range(IDLE_PRODUCTS):
             nc.tensor.matmul(out=idle_acc[:, :P], lhsT=zeros[:], rhs=zeros[:], start=True, stop=True)
 
-        w_scales = keep.tile([P, N_ALL], U8, align_bytes=64)
+        w_scales = keep.tile([P, N_ALL], U8, align_bytes=DMA_ALIGN)
         nc.vector.memset(w_scales[:].bitcast(I32), 0)
 
         ident = keep.tile([P, P], F32)
@@ -60,10 +61,10 @@ def tile_gatedattentionunit_pa_s_kernel(
         nc.scalar.activation(out=warm[:], in_=warm_in[:], func=SILU)
 
         x_rows = hidden_states[0].rearrange("(p t) k -> p t k", t=TT)
-        x_sb = [keep.tile([P, H], BF16, name="x_sb%d" % t) for t in range(TT)]
+        x_sb = [keep.tile([P, H], BF16, name="x_sb%d" % t, align_bytes=DMA_ALIGN) for t in range(TT)]
         for t in range(TT):
             nc.sync.dma_start(out=x_sb[t][:], in_=x_rows[:, t, :])
-        w_words = keep.tile([P, 2 * N_ALL], U8, align_bytes=64)
+        w_words = keep.tile([P, 2 * N_ALL], U8, align_bytes=DMA_ALIGN)
 
         def load_codes(first, last):
             nc.sync.dma_start(
@@ -82,8 +83,8 @@ def tile_gatedattentionunit_pa_s_kernel(
         nc.gpsimd.memset(gain_rows[:], 0.0)
         ones = keep.tile([P, P], BF16)
         nc.gpsimd.memset(ones[:], 1.0)
-        cos_sb = keep.tile([P, TT, HALF], BF16)
-        sin_sb = keep.tile([P, TT, HALF], BF16)
+        cos_sb = keep.tile([P, TT, HALF], BF16, align_bytes=DMA_ALIGN)
+        sin_sb = keep.tile([P, TT, HALF], BF16, align_bytes=DMA_ALIGN)
         nc.sync.dma_start(out=cos_sb[:], in_=cos[0].rearrange("(p t) c -> p t c", t=TT))
         nc.sync.dma_start(out=sin_sb[:], in_=sin[0].rearrange("(p t) c -> p t c", t=TT))
         nc.sync.dma_start(out=gain_rows[0:1, 0:D], in_=q_scale.rearrange("(o c) -> o c", o=1))
@@ -119,7 +120,7 @@ def tile_gatedattentionunit_pa_s_kernel(
         def gated(t, half, c0, width):
             acc = psum_acc.tile([P, BANK], F32, tag="acc")
             project(acc[:, :width], t, half * E + c0, width)
-            stage = stages.tile([P, BANK], F32, tag="stage")
+            stage = stages.tile([P, BANK], F32, tag="stage", align_bytes=DMA_ALIGN)
             nc.scalar.activation(out=stage[:, :width], in_=acc[:, :width], func=SILU)
             rows = (out_0, out_1)[half][0].rearrange("(p t) c -> p t c", t=TT)
             nc.sync.dma_start(out=rows[:, t, c0 : c0 + width], in_=stage[:, :width])
@@ -161,7 +162,7 @@ def tile_gatedattentionunit_pa_s_kernel(
                 in1=gains_all,
                 op=MULT,
             )
-        rotated = keep.tile([P, 2, TT, 2, HALF], F32)
+        rotated = keep.tile([P, 2, TT, 2, HALF], F32, align_bytes=DMA_ALIGN)
         nc.vector.tensor_tensor(
             out=rotated[:, :, :, 0, :].rearrange("p s t c -> p t s c"),
             in0=y_cos[:, :, :, 0, :],

@@ -13,7 +13,6 @@ FP4X4 = mybir.dt.float4_e2m1fn_x4
 SILU = mybir.ActivationFunctionType.Silu
 MULT = mybir.AluOpType.mult
 ADD = mybir.AluOpType.add
-SUBTRACT = mybir.AluOpType.subtract
 
 P = 128
 S = 256
@@ -78,7 +77,6 @@ def tile_gatedattentionunit_pa_s_kernel(
                 in_=W_i_scales[0, 4 * quad : 4 * quad + 4, :].bitcast(I32),
             )
         load_codes(E + NARROW, N_ALL)
-        load_codes(0, E)
         gain_rows = keep.tile([P, 2 * D], BF16)
         nc.gpsimd.memset(gain_rows[:], 0.0)
         ones = keep.tile([P, P], BF16)
@@ -89,6 +87,7 @@ def tile_gatedattentionunit_pa_s_kernel(
         nc.sync.dma_start(out=sin_sb[:], in_=sin[0].rearrange("(p t) c -> p t c", t=TT))
         nc.sync.dma_start(out=gain_rows[0:1, 0:D], in_=q_scale.rearrange("(o c) -> o c", o=1))
         nc.sync.dma_start(out=gain_rows[0:1, D : 2 * D], in_=k_scale.rearrange("(o c) -> o c", o=1))
+        load_codes(0, E)
 
         x_t = [psum_once.tile([P, 2, P], F32, name="x_t%d" % t) for t in range(TT)]
         for t in range(TT):
@@ -126,15 +125,15 @@ def tile_gatedattentionunit_pa_s_kernel(
             nc.sync.dma_start(out=rows[:, t, c0 : c0 + width], in_=stage[:, :width])
 
         gated(0, 1, 0, NARROW)
+        gated(1, 1, 0, NARROW)
+        gated(0, 1, NARROW, BANK)
+        gated(1, 1, NARROW, BANK)
 
         qk_acc = psum_once.tile([P, TT, D], F32)
         for t in range(TT):
             project(qk_acc[:, t, :], t, 2 * E, D)
         qk = keep.tile([P, TT, 2, HALF], F32)
         nc.scalar.activation(out=qk[:], in_=qk_acc[:].rearrange("p t (c e) -> p t e c", e=2), func=SILU)
-
-        gated(0, 1, NARROW, BANK)
-        gated(0, 0, 0, BANK)
 
         gains = psum_once.tile([P, 2, 2, HALF], F32)
         nc.tensor.matmul(
@@ -145,44 +144,41 @@ def tile_gatedattentionunit_pa_s_kernel(
             stop=True,
         )
 
-        y_cos = keep.tile([P, TT, 2, 2, HALF], F32)
-        y_sin = keep.tile([P, TT, 2, 2, HALF], F32)
-        gains_all = gains[:].rearrange("p s e c -> p s (e c)").unsqueeze(1).to_broadcast([P, TT, 2, D])
-        turned = []
-        for name, angle in (("qk_cos", cos_sb), ("qk_sin", sin_sb)):
-            product = keep.tile([P, TT, 2, HALF], F32, name=name)
+        turn = keep.tile([P, TT, 4, HALF], BF16)
+        nc.vector.tensor_copy(out=turn[:, :, 0:4:3, :], in_=cos_sb[:].unsqueeze(2).to_broadcast([P, TT, 2, HALF]))
+        nc.vector.tensor_copy(out=turn[:, :, 2, :], in_=sin_sb[:])
+        nc.vector.tensor_scalar_mul(out=turn[:, :, 1, :], in0=sin_sb[:], scalar1=-1.0)
+        table = keep.tile([P, 2, TT * 2, D], F32)
+        for s in range(2):
             nc.vector.tensor_tensor(
-                out=product[:], in0=qk[:], in1=angle[:].unsqueeze(2).to_broadcast([P, TT, 2, HALF]), op=MULT
-            )
-            turned.append(product)
-        for y, product in zip((y_cos, y_sin), turned):
-            nc.vector.tensor_tensor(
-                out=y[:].rearrange("p t s e c -> p t s (e c)"),
-                in0=product[:].rearrange("p t e c -> p t (e c)").unsqueeze(2).to_broadcast([P, TT, 2, D]),
-                in1=gains_all,
+                out=table[:, s],
+                in0=turn[:].rearrange("p t (h e) c -> p (t h) (e c)", e=2),
+                in1=gains[:, s].rearrange("p e c -> p (e c)").unsqueeze(1).to_broadcast([P, TT * 2, D]),
                 op=MULT,
             )
+        terms = keep.tile([P, 2, TT, 2, D], F32)
         rotated = keep.tile([P, 2, TT, 2, HALF], F32, align_bytes=DMA_ALIGN)
-        nc.vector.tensor_tensor(
-            out=rotated[:, :, :, 0, :].rearrange("p s t c -> p t s c"),
-            in0=y_cos[:, :, :, 0, :],
-            in1=y_sin[:, :, :, 1, :],
-            op=SUBTRACT,
-        )
-        nc.vector.tensor_tensor(
-            out=rotated[:, :, :, 1, :].rearrange("p s t c -> p t s c"),
-            in0=y_sin[:, :, :, 0, :],
-            in1=y_cos[:, :, :, 1, :],
-            op=ADD,
-        )
+        for s in range(2):
+            nc.vector.tensor_tensor(
+                out=terms[:, s],
+                in0=qk[:].rearrange("p t e c -> p t (e c)").unsqueeze(2).to_broadcast([P, TT, 2, D]),
+                in1=table[:, s].rearrange("p (t h) d -> p t h d", h=2),
+                op=MULT,
+            )
+        for s in range(2):
+            nc.vector.tensor_tensor(
+                out=rotated[:, s], in0=terms[:, s, :, :, 0:HALF], in1=terms[:, s, :, :, HALF:D], op=ADD
+            )
 
-        gated(0, 0, BANK, NARROW)
-        gated(1, 1, 0, NARROW)
-        gated(1, 1, NARROW, BANK)
-        gated(1, 0, 0, BANK)
-        for s, out in enumerate((out_2, out_3)):
+        def store_rotated(s):
             nc.sync.dma_start(
-                out=out[0].rearrange("(p t) c -> p (t c)", t=TT),
+                out=(out_2, out_3)[s][0].rearrange("(p t) c -> p (t c)", t=TT),
                 in_=rotated[:, s].rearrange("p t h c -> p (t h c)"),
             )
+
+        gated(0, 0, BANK, NARROW)
+        gated(0, 0, 0, BANK)
+        gated(1, 0, 0, BANK)
+        store_rotated(0)
         gated(1, 0, BANK, NARROW)
+        store_rotated(1)

@@ -38,8 +38,7 @@ def tile_gatedattentionunit_pa_s_kernel(
         ctx.enter_context(tc.manual_schedule())
         keep = ctx.enter_context(tc.tile_pool(name="keep", bufs=1))
         stages = ctx.enter_context(tc.tile_pool(name="stages", bufs=8))
-        psum_once = ctx.enter_context(tc.psum_pool(name="psum_once", bufs=1))
-        psum_acc = ctx.enter_context(tc.psum_pool(name="psum_acc", bufs=4))
+        psum_acc = ctx.enter_context(tc.psum_pool(name="psum_acc", bufs=8))
 
         zeros = keep.tile([P, P], F32)
         nc.vector.memset(zeros[:], 0.0)
@@ -89,7 +88,7 @@ def tile_gatedattentionunit_pa_s_kernel(
         nc.sync.dma_start(out=gain_rows[0:1, D : 2 * D], in_=k_scale.rearrange("(o c) -> o c", o=1))
         load_codes(0, E)
 
-        x_t = [psum_once.tile([P, 2, P], F32, name="x_t%d" % t) for t in range(TT)]
+        x_t = [psum_acc.tile([P, 2, P], F32, name="x_t%d" % t, tag="acc") for t in range(TT)]
         for t in range(TT):
             x_words = x_sb[t][:].bitcast(F32)
             for u in range(2):
@@ -129,13 +128,13 @@ def tile_gatedattentionunit_pa_s_kernel(
         gated(0, 1, NARROW, BANK)
         gated(1, 1, NARROW, BANK)
 
-        qk_acc = psum_once.tile([P, TT, D], F32)
+        qk_acc = psum_acc.tile([P, TT, D], F32, tag="acc")
         for t in range(TT):
             project(qk_acc[:, t, :], t, 2 * E, D)
         qk = keep.tile([P, TT, 2, HALF], F32)
         nc.scalar.activation(out=qk[:], in_=qk_acc[:].rearrange("p t (c e) -> p t e c", e=2), func=SILU)
 
-        gains = psum_once.tile([P, 2, 2, HALF], F32)
+        gains = psum_acc.tile([P, 2, 2, HALF], F32, tag="acc")
         nc.tensor.matmul(
             out=gains[:],
             lhsT=ones[:],

@@ -93,6 +93,7 @@ def tile_gatedattentionunit_pa_s_kernel(
             x_words = x_sb[t][:].bitcast(F32)
             for u in range(2):
                 nc.tensor.transpose(x_t[t][:, u, :], x_words[:, u : H // 2 : 2], ident[:])
+        nc.tensor.matmul(out=idle_acc[:, :P], lhsT=zeros[:], rhs=zeros[:], start=True, stop=True)
         grouped = [keep.tile([P, 4 * P], BF16, name="grouped%d" % t, align_bytes=64) for t in range(TT)]
         for t in range(TT):
             nc.scalar.copy(

@@ -179,6 +179,6 @@ def tile_gatedattentionunit_pa_s_kernel(
         gated(0, 0, BANK, NARROW)
         gated(0, 0, 0, BANK)
         gated(1, 0, 0, BANK)
-        store_rotated(0)
         gated(1, 0, BANK, NARROW)
+        store_rotated(0)
         store_rotated(1)

from contextlib import ExitStack

import concourse.mybir as mybir
from concourse.masks import make_identity

F32 = mybir.dt.float32
BF16 = mybir.dt.bfloat16
I32 = mybir.dt.int32
U32 = mybir.dt.uint32
U8 = mybir.dt.uint8
FP8X4 = mybir.dt.float8_e4m3fn_x4
FP4X4 = mybir.dt.float4_e2m1fn_x4
SILU = mybir.ActivationFunctionType.Silu
MULT = mybir.AluOpType.mult
ADD = mybir.AluOpType.add

P = 128
S = 256
H = 512
E = 768
D = 128
HALF = D // 2
N_ALL = 2 * E + D
TT = S // P
BANK = 512
NARROW = E - BANK
DMA_ALIGN = 256
IDLE_PRODUCTS = 3

FLOPS = 2 * S * H * N_ALL


def tile_gatedattentionunit_pa_s_kernel(
    tc, hidden_states, sin, cos, W_i_words, W_i_scales, q_scale, k_scale, out_0, out_1, out_2, out_3
):
    nc = tc.nc
    with ExitStack() as ctx:
        ctx.enter_context(tc.manual_schedule())
        keep = ctx.enter_context(tc.tile_pool(name="keep", bufs=1))
        stages = ctx.enter_context(tc.tile_pool(name="stages", bufs=8))
        psum_acc = ctx.enter_context(tc.psum_pool(name="psum_acc", bufs=8))

        zeros = keep.tile([P, P], F32)
        nc.vector.memset(zeros[:], 0.0)
        idle_acc = psum_acc.tile([P, BANK], F32, tag="acc")
        for i in range(IDLE_PRODUCTS):
            nc.tensor.matmul(out=idle_acc[:, :P], lhsT=zeros[:], rhs=zeros[:], start=True, stop=True)

        w_scales = keep.tile([P, N_ALL], U8, align_bytes=DMA_ALIGN)
        nc.vector.memset(w_scales[:].bitcast(I32), 0)

        ident = keep.tile([P, P], F32)
        nc.vector.memset(ident[:], 0.0)
        make_identity(nc, ident[:], nomemset=True)

        warm_in = keep.tile([P, 1], F32)
        nc.vector.memset(warm_in[:], 0.0)
        warm = keep.tile([P, 1], F32)
        nc.scalar.activation(out=warm[:], in_=warm_in[:], func=SILU)

        x_rows = hidden_states[0].rearrange("(p t) k -> p t k", t=TT)
        x_sb = [keep.tile([P, H], BF16, name="x_sb%d" % t, align_bytes=DMA_ALIGN) for t in range(TT)]
        for t in range(TT):
            nc.sync.dma_start(out=x_sb[t][:], in_=x_rows[:, t, :])
        w_words = keep.tile([P, 2 * N_ALL], U8, align_bytes=DMA_ALIGN)

        def load_codes(first, last):
            nc.sync.dma_start(
                out=w_words[:, 2 * first : 2 * last].bitcast(I32), in_=W_i_words[0, :, 2 * first : 2 * last].bitcast(I32)
            )

        load_codes(E, E + NARROW)
        for quad in range(4):
            nc.sync.dma_start(
                out=w_scales[32 * quad : 32 * quad + 4, :].bitcast(I32),
                in_=W_i_scales[0, 4 * quad : 4 * quad + 4, :].bitcast(I32),
            )
        load_codes(E + NARROW, N_ALL)
        gain_rows = keep.tile([P, 2 * D], BF16)
        nc.gpsimd.memset(gain_rows[:], 0.0)
        ones = keep.tile([P, P], BF16)
        nc.gpsimd.memset(ones[:], 1.0)
        cos_sb = keep.tile([P, TT, HALF], BF16, align_bytes=DMA_ALIGN)
        sin_sb = keep.tile([P, TT, HALF], BF16, align_bytes=DMA_ALIGN)
        nc.sync.dma_start(out=cos_sb[:], in_=cos[0].rearrange("(p t) c -> p t c", t=TT))
        nc.sync.dma_start(out=sin_sb[:], in_=sin[0].rearrange("(p t) c -> p t c", t=TT))
        nc.sync.dma_start(out=gain_rows[0:1, 0:D], in_=q_scale.rearrange("(o c) -> o c", o=1))
        nc.sync.dma_start(out=gain_rows[0:1, D : 2 * D], in_=k_scale.rearrange("(o c) -> o c", o=1))
        load_codes(0, E)

        x_t = [psum_acc.tile([P, 2, P], F32, name="x_t%d" % t, tag="acc") for t in range(TT)]
        for t in range(TT):
            x_words = x_sb[t][:].bitcast(F32)
            for u in range(2):
                nc.tensor.transpose(x_t[t][:, u, :], x_words[:, u : H // 2 : 2], ident[:])
        nc.tensor.matmul(out=idle_acc[:, :P], lhsT=zeros[:], rhs=zeros[:], start=True, stop=True)
        grouped = [keep.tile([P, 4 * P], BF16, name="grouped%d" % t, align_bytes=64) for t in range(TT)]
        for t in range(TT):
            nc.scalar.copy(
                out=grouped[t][:].bitcast(F32).rearrange("p (r u) -> p r u", u=2),
                in_=x_t[t][:].rearrange("p u r -> p r u"),
            )
        x_codes = keep.tile([P, TT, P], U32, align_bytes=64)
        x_scales = keep.tile([P, TT, P], U8, align_bytes=64)
        for t in range(TT):
            nc.vector.quantize_mx(out=x_codes[:, t, :].bitcast(FP8X4), scales=x_scales[:, t, :], in_=grouped[t][:])

        def project(acc, t, first, width):
            nc.tensor.matmul_mx(
                out=acc,
                lhsT=x_codes[:, t, :].bitcast(FP8X4),
                lhsT_scale=x_scales[:, t, :],
                rhs=w_words[:, 2 * first : 2 * (first + width)].bitcast(FP4X4),
                rhs_scale=w_scales[:, first : first + width],
                start=True,
                stop=True,
            )

        def gated(t, half, c0, width):
            acc = psum_acc.tile([P, BANK], F32, tag="acc")
            project(acc[:, :width], t, half * E + c0, width)
            stage = stages.tile([P, BANK], F32, tag="stage", align_bytes=DMA_ALIGN)
            nc.scalar.activation(out=stage[:, :width], in_=acc[:, :width], func=SILU)
            rows = (out_0, out_1)[half][0].rearrange("(p t) c -> p t c", t=TT)
            nc.sync.dma_start(out=rows[:, t, c0 : c0 + width], in_=stage[:, :width])

        gated(0, 1, 0, NARROW)
        gated(1, 1, 0, NARROW)
        gated(0, 1, NARROW, BANK)
        gated(1, 1, NARROW, BANK)

        qk_acc = psum_acc.tile([P, TT, D], F32, tag="acc")
        for t in range(TT):
            project(qk_acc[:, t, :], t, 2 * E, D)
        qk = keep.tile([P, TT, 2, HALF], F32)
        nc.scalar.activation(out=qk[:], in_=qk_acc[:].rearrange("p t (c e) -> p t e c", e=2), func=SILU)

        gains = psum_acc.tile([P, 2, 2, HALF], F32, tag="acc")
        nc.tensor.matmul(
            out=gains[:],
            lhsT=ones[:],
            rhs=gain_rows[:].rearrange("p (s c e) -> p s e c", s=2, e=2),
            start=True,
            stop=True,
        )

        turn = keep.tile([P, TT, 4, HALF], BF16)
        nc.vector.tensor_copy(out=turn[:, :, 0:4:3, :], in_=cos_sb[:].unsqueeze(2).to_broadcast([P, TT, 2, HALF]))
        nc.vector.tensor_copy(out=turn[:, :, 2, :], in_=sin_sb[:])
        nc.vector.tensor_scalar_mul(out=turn[:, :, 1, :], in0=sin_sb[:], scalar1=-1.0)
        table = keep.tile([P, 2, TT * 2, D], F32)
        for s in range(2):
            nc.vector.tensor_tensor(
                out=table[:, s],
                in0=turn[:].rearrange("p t (h e) c -> p (t h) (e c)", e=2),
                in1=gains[:, s].rearrange("p e c -> p (e c)").unsqueeze(1).to_broadcast([P, TT * 2, D]),
                op=MULT,
            )
        terms = keep.tile([P, 2, TT, 2, D], F32)
        rotated = keep.tile([P, 2, TT, 2, HALF], F32, align_bytes=DMA_ALIGN)
        for s in range(2):
            nc.vector.tensor_tensor(
                out=terms[:, s],
                in0=qk[:].rearrange("p t e c -> p t (e c)").unsqueeze(2).to_broadcast([P, TT, 2, D]),
                in1=table[:, s].rearrange("p (t h) d -> p t h d", h=2),
                op=MULT,
            )
        for s in range(2):
            nc.vector.tensor_tensor(
                out=rotated[:, s], in0=terms[:, s, :, :, 0:HALF], in1=terms[:, s, :, :, HALF:D], op=ADD
            )

        def store_rotated(s):
            nc.sync.dma_start(
                out=(out_2, out_3)[s][0].rearrange("(p t) c -> p (t c)", t=TT),
                in_=rotated[:, s].rearrange("p t h c -> p (t h c)"),
            )

        gated(0, 0, BANK, NARROW)
        gated(0, 0, 0, BANK)
        gated(1, 0, 0, BANK)
        gated(1, 0, BANK, NARROW)
        store_rotated(0)
        store_rotated(1)
